import numpy as np
import ml_dtypes


BF16 = ml_dtypes.bfloat16


def bf(x):
    return np.asarray(x, np.float32).astype(BF16)


def f64(x):
    return np.asarray(x).astype(np.float64)


E2M1 = np.array([0.0, 0.5, 1.0, 1.5, 2.0, 3.0, 4.0, 6.0, -0.0, -0.5, -1.0, -1.5, -2.0, -3.0, -4.0, -6.0])


def pack_weight(w, fmt):
    k, n = w.shape
    w = f64(bf(w)).reshape(k // 32, 32, n)
    amax = np.abs(w).max(1)
    if fmt == "e4m3":
        byte = np.frexp(amax)[1] - 1 + 127 - 7
    else:
        mant, ex = np.frexp(amax / 6.0)
        byte = np.where(mant > 0.5, ex, ex - 1) + 127
    byte = np.clip(np.where(amax > 0, byte, 1), 1, 254)
    scaled = (w * np.exp2(127.0 - byte)[:, None, :]).reshape(k, n).astype(np.float32)
    by_word = np.ascontiguousarray(scaled.reshape(k // 512, 128, 4, n).transpose(0, 1, 3, 2))
    if fmt == "e4m3":
        words = by_word.astype(ml_dtypes.float8_e4m3fn).view(np.uint8)
    else:
        c = by_word.astype(ml_dtypes.float4_e2m1fn).view(np.uint8) & 0xF
        words = c[..., 0::2] | (c[..., 1::2] << 4)
    return np.ascontiguousarray(words), np.ascontiguousarray(byte.astype(np.uint8).reshape(k // 512, 16, n))


def unpack_weight(words, scales, fmt):
    g, p, n, _ = words.shape
    if fmt == "e4m3":
        vals = np.ascontiguousarray(words).view(ml_dtypes.float8_e4m3fn).astype(np.float64)
    else:
        nib = np.empty((g, p, n, 4), np.uint8)
        nib[..., 0::2] = words & 0xF
        nib[..., 1::2] = words >> 4
        vals = E2M1[nib]
    vals = vals * np.repeat(np.exp2(scales.astype(np.float64) - 127.0), 8, axis=1)[..., None]
    return vals.transpose(0, 1, 3, 2).reshape(g * 512, n)

def pack4(w):
    words, scales = pack_weight(w, "e2m1")
    return words.reshape(words.shape[0], 128, -1), scales


def unpack4(words, scales):
    return unpack_weight(words.reshape(words.shape[0], 128, -1, 2), scales, "e2m1")


def kspread(k):
    return np.exp2(np.repeat(np.random.randint(-6, 7, k // 32), 32).astype(np.float64))


B, T, H, HD = 2, 64, 16, 256
D = H * HD
HALF = HD // 2
ROPE_BASE = 10000.0


def to_heads(t):
    return t.reshape(B, T, H, HD).transpose(0, 2, 1, 3)


def rotate(t, cos, sin):
    t1, t2 = t[..., :HALF], t[..., HALF:]
    c = cos[None, None, :, :]
    s = sin[None, None, :, :]
    return np.concatenate([t1 * c - t2 * s, t1 * s + t2 * c], axis=-1)


def setup_inputs():
    s = kspread(D)
    inv_freq = 1.0 / (ROPE_BASE ** (np.arange(0, HD, 2) / HD))
    ang = np.arange(T)[:, None] * inv_freq[None, :]
    x = np.random.standard_normal((B, T, D)) * s
    x_words, x_scales = pack4(np.ascontiguousarray(x.reshape(B * T, D).T))
    Wqk = np.random.standard_normal((2 * D, D)) * D ** -0.5 / s[None, :]
    words, scales = pack4(np.ascontiguousarray(Wqk.T))
    return {"x_words": x_words,
            "x_scales": x_scales,
            "Wqk_words": words,
            "Wqk_scales": scales,
            "bqk": bf(np.random.standard_normal(2 * D) * 0.3),
            "cos": bf(np.cos(ang)),
            "sin": bf(np.sin(ang))}


def reference(x_words, x_scales, Wqk_words, Wqk_scales, bqk, cos, sin):
    xv = unpack4(x_words, x_scales).T.reshape(B, T, D)
    qk = (xv @ unpack4(Wqk_words, Wqk_scales)) + f64(bqk)
    q, k = np.split(qk, 2, axis=-1)
    q, k = to_heads(q), to_heads(k)
    return rotate(q, f64(cos), f64(sin)), rotate(k, f64(cos), f64(sin))

@@ -1,0 +1,214 @@
+from contextlib import ExitStack
+
+import concourse.mybir as mybir
+from concourse.masks import make_identity
+
+FLOPS = 2 * 128 * 4096 * 8192
+
+F32 = mybir.dt.float32
+BF16 = mybir.dt.bfloat16
+I32 = mybir.dt.int32
+U8 = mybir.dt.uint8
+FP4X4 = mybir.dt.float4_e2m1fn_x4
+ADD = mybir.AluOpType.add
+MULT = mybir.AluOpType.mult
+
+P = 128
+PASSES = 8
+BANK = 512
+HALF = 128
+HEAD = 256
+NCOLS = 8192
+SUPER = 2048
+N_SUPER = NCOLS // SUPER
+N_SLOTS = 3
+UNIT = 1024
+CHUNK_BYTES = 8192
+
+SUBGROUPS = (
+    ((0, 4, (2, 2, 2, 2)),),
+    ((0, 4, (2, 2, 2, 2)),),
+    ((0, 4, (2, 2, 2, 2)),),
+    ((0, 2, (4, 4)), (2, 1, (8,)), (3, 1, (4, 4))),
+)
+
+
+def tile_selfattention_pa_kernel(tc, x_words, x_scales, Wqk_words, Wqk_scales, bqk, cos, sin, out_0, out_1):
+    nc = tc.nc
+    outs = (out_0, out_1)
+
+    with ExitStack() as ctx:
+        const = ctx.enter_context(tc.tile_pool(name="const", bufs=1))
+        codes_pool = ctx.enter_context(tc.tile_pool(name="codes", bufs=12))
+        work = ctx.enter_context(tc.tile_pool(name="work", bufs=2))
+        outp = ctx.enter_context(tc.tile_pool(name="outp", bufs=4))
+        psum = ctx.enter_context(tc.psum_pool(name="psum", bufs=8))
+        ctx.enter_context(tc.manual_schedule())
+
+        warm_in = const.tile([P, 8], F32, name="warm_in")
+        warm_out = const.tile([P, 8], F32, name="warm_out")
+        x_codes_in = const.tile([P, PASSES, 2 * P], U8, name="x_codes_in", align_bytes=64)
+        x_plane_in = const.tile([P, PASSES, P], U8, name="x_plane_in", align_bytes=64)
+        x_codes = const.tile([P, PASSES, 2 * P], U8, name="x_codes", align_bytes=64)
+        x_plane = const.tile([P, PASSES, P], U8, name="x_plane", align_bytes=64)
+        slots = []
+        for i in range(N_SLOTS):
+            slot = const.tile([P, PASSES, SUPER], U8, name="slot%d" % i, align_bytes=64)
+            slots.append(slot)
+        bias_rows = const.tile([P, BANK], BF16, name="bias_rows")
+        ident = const.tile([P, P], BF16, name="ident")
+        cs = const.tile([P, 2, HALF], BF16, name="cs")
+        cos_t = const.tile([P, UNIT], F32, name="cos_t")
+        sin_t = const.tile([P, UNIT], F32, name="sin_t")
+        bias_sb = const.tile([P, NCOLS], BF16, name="bias_sb")
+
+        def load_scales(plane, src, c0, width):
+            for r in range(4):
+                nc.sync.dma_start(
+                    out=plane[r:P:32, :, 0:width].bitcast(I32),
+                    in_=src[:, r:16:4, c0 : c0 + width].rearrange("g q n -> q g n").bitcast(I32),
+                )
+
+        def load_codes(c0, width, g0, n_g):
+            ct = codes_pool.tile([P, CHUNK_BYTES], U8, name="ct", tag="ct", align_bytes=64)
+            view = ct[:, 0 : n_g * 2 * width].rearrange("p (g c) -> p g c", g=n_g)
+            nc.sync.dma_start(
+                out=view.bitcast(I32),
+                in_=Wqk_words[g0 : g0 + n_g, :, 2 * c0 : 2 * (c0 + width)].rearrange("g p c -> p g c").bitcast(I32),
+            )
+            return view
+
+        loaded = {}
+
+        def load_super(s, first_chunk_done):
+            load_scales(slots[s % N_SLOTS], Wqk_scales, SUPER * s, SUPER)
+            for q, (b0, nb, chunks) in enumerate(SUBGROUPS[s]):
+                g0 = 0
+                for ci, n_g in enumerate(chunks):
+                    if not (first_chunk_done and q == 0 and ci == 0):
+                        loaded[(s, q, ci)] = load_codes(SUPER * s + BANK * b0, BANK * nb, g0, n_g)
+                    g0 += n_g
+
+        nc.vector.memset(warm_in[:], 0.0)
+        nc.scalar.copy(out=warm_out[:], in_=warm_in[:])
+        nc.vector.memset(x_plane_in[:].bitcast(I32), 0)
+        nc.vector.memset(slots[0][:].bitcast(I32), 0)
+        nc.gpsimd.memset(bias_rows[:], 0.0)
+        make_identity(nc, ident[:])
+        nc.gpsimd.memset(slots[1][:].bitcast(F32), 0.0)
+        nc.gpsimd.memset(slots[2][:].bitcast(F32), 0.0)
+
+        nc.scalar.dma_start(out=bias_rows[0:16, :], in_=bqk.rearrange("(j n) -> j n", n=BANK))
+        for b in range(2):
+            nc.scalar.dma_start(out=cs[b:P:2, 0, :], in_=cos)
+            nc.scalar.dma_start(out=cs[b:P:2, 1, :], in_=sin)
+
+        nc.sync.dma_start(out=x_codes_in[:].bitcast(I32), in_=x_words.rearrange("g p c -> p g c").bitcast(I32))
+        b0, nb, chunks = SUBGROUPS[0][0]
+        loaded[(0, 0, 0)] = load_codes(BANK * b0, BANK * nb, 0, chunks[0])
+        load_scales(x_plane_in, x_scales, 0, P)
+        load_super(0, True)
+        load_super(1, False)
+
+        for b in range(2):
+            nc.vector.tensor_copy(
+                out=x_codes[:].rearrange("p g (t b e) -> p g t b e", b=2, e=2)[:, :, :, b, :],
+                in_=x_codes_in[:].rearrange("p g (b t e) -> p g b t e", b=2, e=2)[:, :, b, :, :],
+            )
+            nc.vector.tensor_copy(
+                out=x_plane[:].rearrange("p g (t b) -> p g t b", b=2)[:, :, :, b],
+                in_=x_plane_in[:].rearrange("p g (b t) -> p g b t", b=2)[:, :, b, :],
+            )
+
+        nc.vector.tensor_copy(out=cos_t[:, 0:HALF], in_=cs[:, 0, :])
+        nc.vector.tensor_copy(out=sin_t[:, 0:HALF], in_=cs[:, 1, :])
+        nc.vector.tensor_copy(out=cos_t[:, HALF:HEAD], in_=cs[:, 0, :])
+        nc.vector.tensor_scalar_mul(out=sin_t[:, HALF:HEAD], in0=cs[:, 1, :], scalar1=-1.0)
+        for n in (HEAD, 2 * HEAD):
+            nc.vector.tensor_copy(out=cos_t[:, n : 2 * n], in_=cos_t[:, 0:n])
+            nc.vector.tensor_copy(out=sin_t[:, n : 2 * n], in_=sin_t[:, 0:n])
+
+        def spread_bias(m):
+            bp = psum.tile([P, 2 * BANK], BF16, name="bp", tag="bank")
+            for e in range(2):
+                j = 2 * m + e
+                nc.tensor.matmul(
+                    out=bp[:, BANK * e : BANK * (e + 1)],
+                    lhsT=ident[:, j : j + 1].to_broadcast([P, P]),
+                    rhs=bias_rows[:],
+                    start=True,
+                    stop=True,
+                )
+            nc.scalar.copy(out=bias_sb[:, 2 * BANK * m : 2 * BANK * (m + 1)], in_=bp[:])
+
+        spread_bias(0)
+        spread_bias(1)
+
+        def rotate_and_store(c0, accs):
+            nb = len(accs)
+            per_unit = 2 if nb == 4 else 1
+            units = []
+            for k0 in range(0, nb, per_unit):
+                u = work.tile([P, UNIT], F32, name="u", tag="u")
+                for k in range(per_unit):
+                    col = c0 + BANK * (k0 + k)
+                    nc.vector.tensor_tensor(
+                        out=u[:, BANK * k : BANK * (k + 1)],
+                        in0=accs[k0 + k][:],
+                        in1=bias_sb[:, col : col + BANK],
+                        op=ADD,
+                    )
+                units.append((c0 + BANK * k0, u))
+            n = BANK * per_unit
+            prods = []
+            for col, u in units:
+                v = work.tile([P, UNIT], F32, name="v", tag="v")
+                w = work.tile([P, UNIT], F32, name="w", tag="w")
+                nc.vector.tensor_tensor(out=v[:, 0:n], in0=u[:, 0:n], in1=cos_t[:, 0:n], op=MULT)
+                nc.vector.tensor_tensor(out=w[:, 0:n], in0=u[:, 0:n], in1=sin_t[:, 0:n], op=MULT)
+                prods.append((col, v, w))
+            for col, v, w in prods:
+                o = outp.tile([P, UNIT], F32, name="o", tag="o")
+                v4 = v[:, 0:n].rearrange("p (h s f) -> p h s f", s=2, f=HALF)
+                w4 = w[:, 0:n].rearrange("p (h s f) -> p h s f", s=2, f=HALF)
+                o4 = o[:, 0:n].rearrange("p (h s f) -> p h s f", s=2, f=HALF)
+                nc.vector.tensor_tensor(out=o4[:, :, 0, :], in0=v4[:, :, 0, :], in1=w4[:, :, 1, :], op=ADD)
+                nc.vector.tensor_tensor(out=o4[:, :, 1, :], in0=v4[:, :, 1, :], in1=w4[:, :, 0, :], op=ADD)
+                dst = outs[col // (NCOLS // 2)]
+                h0 = (col % (NCOLS // 2)) // HEAD
+                n_h = n // HEAD
+                for h in range(n_h):
+                    queue = nc.scalar if (h % 2 == 0 or col + n == NCOLS) else nc.gpsimd
+                    queue.dma_start(
+                        out=dst[:, h0 + h, :, :].rearrange("b t f -> t b f"),
+                        in_=o[:, HEAD * h : HEAD * (h + 1)],
+                    )
+
+        for s in range(N_SUPER):
+            if s + 2 < N_SUPER:
+                load_super(s + 2, False)
+            plane = slots[s % N_SLOTS]
+            for q, (b0, nb, chunks) in enumerate(SUBGROUPS[s]):
+                if q == 0 and s + 1 < N_SUPER:
+                    spread_bias(2 * s + 2)
+                    spread_bias(2 * s + 3)
+                accs = []
+                for k in range(nb):
+                    acc = psum.tile([P, BANK], F32, name="acc", tag="bank")
+                    accs.append(acc)
+                g = 0
+                for ci, n_g in enumerate(chunks):
+                    view = loaded[(s, q, ci)]
+                    for gi in range(n_g):
+                        for k in range(nb):
+                            nc.tensor.matmul_mx(
+                                out=accs[k][:],
+                                lhsT=x_codes[:, g, :].bitcast(FP4X4),
+                                lhsT_scale=x_plane[:, g, :],
+                                rhs=view[:, gi, 2 * BANK * k : 2 * BANK * (k + 1)].bitcast(FP4X4),
+                                rhs_scale=plane[:, g, BANK * (b0 + k) : BANK * (b0 + k + 1)],
+                                start=(g == 0),
+                                stop=(g == PASSES - 1),
+                            )
+                        g += 1
+                rotate_and_store(SUPER * s + BANK * b0, accs)

@@ -39,9 +39,9 @@ def tile_selfattention_pa_kernel(tc, x_words, x_scales, Wqk_words, Wqk_scales, b
 
     with ExitStack() as ctx:
         const = ctx.enter_context(tc.tile_pool(name="const", bufs=1))
-        codes_pool = ctx.enter_context(tc.tile_pool(name="codes", bufs=12))
+        codes_pool = ctx.enter_context(tc.tile_pool(name="codes", bufs=6))
         work = ctx.enter_context(tc.tile_pool(name="work", bufs=2))
-        outp = ctx.enter_context(tc.tile_pool(name="outp", bufs=4))
+        outp = ctx.enter_context(tc.tile_pool(name="outp", bufs=6))
         psum = ctx.enter_context(tc.psum_pool(name="psum", bufs=8))
         ctx.enter_context(tc.manual_schedule())
 
@@ -62,11 +62,11 @@ def tile_selfattention_pa_kernel(tc, x_words, x_scales, Wqk_words, Wqk_scales, b
         sin_t = const.tile([P, UNIT], F32, name="sin_t")
         bias_sb = const.tile([P, NCOLS], BF16, name="bias_sb")
 
-        def load_scales(plane, src, c0, width):
+        def load_scales(queue, word, plane, src, c0, width):
             for r in range(4):
-                nc.sync.dma_start(
-                    out=plane[r:P:32, :, 0:width].bitcast(I32),
-                    in_=src[:, r:16:4, c0 : c0 + width].rearrange("g q n -> q g n").bitcast(I32),
+                queue.dma_start(
+                    out=plane[r:P:32, :, 0:width].bitcast(word),
+                    in_=src[:, r:16:4, c0 : c0 + width].rearrange("g q n -> q g n").bitcast(word),
                 )
 
         def load_codes(c0, width, g0, n_g):
@@ -81,7 +81,7 @@ def tile_selfattention_pa_kernel(tc, x_words, x_scales, Wqk_words, Wqk_scales, b
         loaded = {}
 
         def load_super(s, first_chunk_done):
-            load_scales(slots[s % N_SLOTS], Wqk_scales, SUPER * s, SUPER)
+            load_scales(nc.gpsimd, F32, slots[s % N_SLOTS], Wqk_scales, SUPER * s, SUPER)
             for q, (b0, nb, chunks) in enumerate(SUBGROUPS[s]):
                 g0 = 0
                 for ci, n_g in enumerate(chunks):
@@ -95,8 +95,6 @@ def tile_selfattention_pa_kernel(tc, x_words, x_scales, Wqk_words, Wqk_scales, b
         nc.vector.memset(slots[0][:].bitcast(I32), 0)
         nc.gpsimd.memset(bias_rows[:], 0.0)
         make_identity(nc, ident[:])
-        nc.gpsimd.memset(slots[1][:].bitcast(F32), 0.0)
-        nc.gpsimd.memset(slots[2][:].bitcast(F32), 0.0)
 
         nc.scalar.dma_start(out=bias_rows[0:16, :], in_=bqk.rearrange("(j n) -> j n", n=BANK))
         for b in range(2):
@@ -106,9 +104,8 @@ def tile_selfattention_pa_kernel(tc, x_words, x_scales, Wqk_words, Wqk_scales, b
         nc.sync.dma_start(out=x_codes_in[:].bitcast(I32), in_=x_words.rearrange("g p c -> p g c").bitcast(I32))
         b0, nb, chunks = SUBGROUPS[0][0]
         loaded[(0, 0, 0)] = load_codes(BANK * b0, BANK * nb, 0, chunks[0])
-        load_scales(x_plane_in, x_scales, 0, P)
+        load_scales(nc.sync, I32, x_plane_in, x_scales, 0, P)
         load_super(0, True)
-        load_super(1, False)
 
         for b in range(2):
             nc.vector.tensor_copy(
@@ -120,6 +117,9 @@ def tile_selfattention_pa_kernel(tc, x_words, x_scales, Wqk_words, Wqk_scales, b
                 in_=x_plane_in[:].rearrange("p g (b t) -> p g b t", b=2)[:, :, b, :],
             )
 
+        nc.vector.memset(slots[1][:].bitcast(I32), 0)
+        load_super(1, False)
+
         nc.vector.tensor_copy(out=cos_t[:, 0:HALF], in_=cs[:, 0, :])
         nc.vector.tensor_copy(out=sin_t[:, 0:HALF], in_=cs[:, 1, :])
         nc.vector.tensor_copy(out=cos_t[:, HALF:HEAD], in_=cs[:, 0, :])
@@ -127,6 +127,8 @@ def tile_selfattention_pa_kernel(tc, x_words, x_scales, Wqk_words, Wqk_scales, b
         for n in (HEAD, 2 * HEAD):
             nc.vector.tensor_copy(out=cos_t[:, n : 2 * n], in_=cos_t[:, 0:n])
             nc.vector.tensor_copy(out=sin_t[:, n : 2 * n], in_=sin_t[:, 0:n])
+
+        nc.vector.memset(slots[2][:].bitcast(I32), 0)
 
         def spread_bias(m):
             bp = psum.tile([P, 2 * BANK], BF16, name="bp", tag="bank")
@@ -178,8 +180,7 @@ def tile_selfattention_pa_kernel(tc, x_words, x_scales, Wqk_words, Wqk_scales, b
                 h0 = (col % (NCOLS // 2)) // HEAD
                 n_h = n // HEAD
                 for h in range(n_h):
-                    queue = nc.scalar if (h % 2 == 0 or col + n == NCOLS) else nc.gpsimd
-                    queue.dma_start(
+                    nc.scalar.dma_start(
                         out=dst[:, h0 + h, :, :].rearrange("b t f -> t b f"),
                         in_=o[:, HEAD * h : HEAD * (h + 1)],
                     )

@@ -39,9 +39,9 @@ def tile_selfattention_pa_kernel(tc, x_words, x_scales, Wqk_words, Wqk_scales, b
 
     with ExitStack() as ctx:
         const = ctx.enter_context(tc.tile_pool(name="const", bufs=1))
-        codes_pool = ctx.enter_context(tc.tile_pool(name="codes", bufs=6))
+        codes_pool = ctx.enter_context(tc.tile_pool(name="codes", bufs=8))
         work = ctx.enter_context(tc.tile_pool(name="work", bufs=2))
-        outp = ctx.enter_context(tc.tile_pool(name="outp", bufs=6))
+        outp = ctx.enter_context(tc.tile_pool(name="outp", bufs=1))
         psum = ctx.enter_context(tc.psum_pool(name="psum", bufs=8))
         ctx.enter_context(tc.manual_schedule())
 
@@ -62,11 +62,11 @@ def tile_selfattention_pa_kernel(tc, x_words, x_scales, Wqk_words, Wqk_scales, b
         sin_t = const.tile([P, UNIT], F32, name="sin_t")
         bias_sb = const.tile([P, NCOLS], BF16, name="bias_sb")
 
-        def load_scales(queue, word, plane, src, c0, width):
+        def load_scales(plane, src, c0, width):
             for r in range(4):
-                queue.dma_start(
-                    out=plane[r:P:32, :, 0:width].bitcast(word),
-                    in_=src[:, r:16:4, c0 : c0 + width].rearrange("g q n -> q g n").bitcast(word),
+                nc.sync.dma_start(
+                    out=plane[r:P:32, :, 0:width].bitcast(I32),
+                    in_=src[:, r:16:4, c0 : c0 + width].rearrange("g q n -> q g n").bitcast(I32),
                 )
 
         def load_codes(c0, width, g0, n_g):
@@ -81,7 +81,7 @@ def tile_selfattention_pa_kernel(tc, x_words, x_scales, Wqk_words, Wqk_scales, b
         loaded = {}
 
         def load_super(s, first_chunk_done):
-            load_scales(nc.gpsimd, F32, slots[s % N_SLOTS], Wqk_scales, SUPER * s, SUPER)
+            load_scales(slots[s % N_SLOTS], Wqk_scales, SUPER * s, SUPER)
             for q, (b0, nb, chunks) in enumerate(SUBGROUPS[s]):
                 g0 = 0
                 for ci, n_g in enumerate(chunks):
@@ -95,6 +95,8 @@ def tile_selfattention_pa_kernel(tc, x_words, x_scales, Wqk_words, Wqk_scales, b
         nc.vector.memset(slots[0][:].bitcast(I32), 0)
         nc.gpsimd.memset(bias_rows[:], 0.0)
         make_identity(nc, ident[:])
+        nc.gpsimd.memset(slots[1][:].bitcast(F32), 0.0)
+        nc.gpsimd.memset(slots[2][:].bitcast(F32), 0.0)
 
         nc.scalar.dma_start(out=bias_rows[0:16, :], in_=bqk.rearrange("(j n) -> j n", n=BANK))
         for b in range(2):
@@ -104,8 +106,9 @@ def tile_selfattention_pa_kernel(tc, x_words, x_scales, Wqk_words, Wqk_scales, b
         nc.sync.dma_start(out=x_codes_in[:].bitcast(I32), in_=x_words.rearrange("g p c -> p g c").bitcast(I32))
         b0, nb, chunks = SUBGROUPS[0][0]
         loaded[(0, 0, 0)] = load_codes(BANK * b0, BANK * nb, 0, chunks[0])
-        load_scales(nc.sync, I32, x_plane_in, x_scales, 0, P)
+        load_scales(x_plane_in, x_scales, 0, P)
         load_super(0, True)
+        load_super(1, False)
 
         for b in range(2):
             nc.vector.tensor_copy(
@@ -117,9 +120,6 @@ def tile_selfattention_pa_kernel(tc, x_words, x_scales, Wqk_words, Wqk_scales, b
                 in_=x_plane_in[:].rearrange("p g (b t) -> p g b t", b=2)[:, :, b, :],
             )
 
-        nc.vector.memset(slots[1][:].bitcast(I32), 0)
-        load_super(1, False)
-
         nc.vector.tensor_copy(out=cos_t[:, 0:HALF], in_=cs[:, 0, :])
         nc.vector.tensor_copy(out=sin_t[:, 0:HALF], in_=cs[:, 1, :])
         nc.vector.tensor_copy(out=cos_t[:, HALF:HEAD], in_=cs[:, 0, :])
@@ -127,8 +127,6 @@ def tile_selfattention_pa_kernel(tc, x_words, x_scales, Wqk_words, Wqk_scales, b
         for n in (HEAD, 2 * HEAD):
             nc.vector.tensor_copy(out=cos_t[:, n : 2 * n], in_=cos_t[:, 0:n])
             nc.vector.tensor_copy(out=sin_t[:, n : 2 * n], in_=sin_t[:, 0:n])
-
-        nc.vector.memset(slots[2][:].bitcast(I32), 0)
 
         def spread_bias(m):
             bp = psum.tile([P, 2 * BANK], BF16, name="bp", tag="bank")
@@ -145,6 +143,8 @@ def tile_selfattention_pa_kernel(tc, x_words, x_scales, Wqk_words, Wqk_scales, b
 
         spread_bias(0)
         spread_bias(1)
+
+        pending = []
 
         def rotate_and_store(c0, accs):
             nb = len(accs)
@@ -170,7 +170,7 @@ def tile_selfattention_pa_kernel(tc, x_words, x_scales, Wqk_words, Wqk_scales, b
                 nc.vector.tensor_tensor(out=w[:, 0:n], in0=u[:, 0:n], in1=sin_t[:, 0:n], op=MULT)
                 prods.append((col, v, w))
             for col, v, w in prods:
-                o = outp.tile([P, UNIT], F32, name="o", tag="o")
+                o = outp.tile([P, n], F32, name="o%d" % col)
                 v4 = v[:, 0:n].rearrange("p (h s f) -> p h s f", s=2, f=HALF)
                 w4 = w[:, 0:n].rearrange("p (h s f) -> p h s f", s=2, f=HALF)
                 o4 = o[:, 0:n].rearrange("p (h s f) -> p h s f", s=2, f=HALF)
@@ -180,10 +180,7 @@ def tile_selfattention_pa_kernel(tc, x_words, x_scales, Wqk_words, Wqk_scales, b
                 h0 = (col % (NCOLS // 2)) // HEAD
                 n_h = n // HEAD
                 for h in range(n_h):
-                    nc.scalar.dma_start(
-                        out=dst[:, h0 + h, :, :].rearrange("b t f -> t b f"),
-                        in_=o[:, HEAD * h : HEAD * (h + 1)],
-                    )
+                    pending.append((dst[:, h0 + h, :, :].rearrange("b t f -> t b f"), o[:, HEAD * h : HEAD * (h + 1)]))
 
         for s in range(N_SUPER):
             if s + 2 < N_SUPER:
@@ -213,3 +210,6 @@ def tile_selfattention_pa_kernel(tc, x_words, x_scales, Wqk_words, Wqk_scales, b
                             )
                         g += 1
                 rotate_and_store(SUPER * s + BANK * b0, accs)
+
+        for dst_ap, src_ap in pending:
+            nc.sync.dma_start(out=dst_ap, in_=src_ap)

@@ -42,7 +42,8 @@ def tile_selfattention_pa_kernel(tc, x_words, x_scales, Wqk_words, Wqk_scales, b
         codes_pool = ctx.enter_context(tc.tile_pool(name="codes", bufs=8))
         work = ctx.enter_context(tc.tile_pool(name="work", bufs=2))
         outp = ctx.enter_context(tc.tile_pool(name="outp", bufs=1))
-        psum = ctx.enter_context(tc.psum_pool(name="psum", bufs=8))
+        psum = ctx.enter_context(tc.psum_pool(name="psum", bufs=7))
+        psum_warm = ctx.enter_context(tc.psum_pool(name="psum_warm", bufs=1))
         ctx.enter_context(tc.manual_schedule())
 
         warm_in = const.tile([P, 8], F32, name="warm_in")
@@ -145,6 +146,8 @@ def tile_selfattention_pa_kernel(tc, x_words, x_scales, Wqk_words, Wqk_scales, b
         spread_bias(1)
 
         pending = []
+        warm_ps = psum_warm.tile([P, BANK], F32, name="warm_ps")
+        n_mx = 0
 
         def rotate_and_store(c0, accs):
             nb = len(accs)
@@ -208,6 +211,15 @@ def tile_selfattention_pa_kernel(tc, x_words, x_scales, Wqk_words, Wqk_scales, b
                                 start=(g == 0),
                                 stop=(g == PASSES - 1),
                             )
+                            n_mx += 1
+                            if n_mx % 4 == 0:
+                                nc.tensor.matmul(
+                                    out=warm_ps[:, 0:HEAD],
+                                    lhsT=cos_t[:, 0:P],
+                                    rhs=cos_t[:, 0:HEAD],
+                                    start=True,
+                                    stop=True,
+                                )
                         g += 1
                 rotate_and_store(SUPER * s + BANK * b0, accs)
 

@@ -29,21 +29,19 @@ SUBGROUPS = (
     ((0, 4, (2, 2, 2, 2)),),
     ((0, 4, (2, 2, 2, 2)),),
     ((0, 4, (2, 2, 2, 2)),),
-    ((0, 2, (4, 4)), (2, 1, (8,)), (3, 1, (4, 4))),
+    ((0, 1, (8,)), (1, 1, (8,)), (2, 1, (8,)), (3, 1, (4, 3, 1))),
 )
 
 
 def tile_selfattention_pa_kernel(tc, x_words, x_scales, Wqk_words, Wqk_scales, bqk, cos, sin, out_0, out_1):
     nc = tc.nc
-    outs = (out_0, out_1)
 
     with ExitStack() as ctx:
         const = ctx.enter_context(tc.tile_pool(name="const", bufs=1))
         codes_pool = ctx.enter_context(tc.tile_pool(name="codes", bufs=8))
         work = ctx.enter_context(tc.tile_pool(name="work", bufs=2))
         outp = ctx.enter_context(tc.tile_pool(name="outp", bufs=1))
-        psum = ctx.enter_context(tc.psum_pool(name="psum", bufs=7))
-        psum_warm = ctx.enter_context(tc.psum_pool(name="psum_warm", bufs=1))
+        psum = ctx.enter_context(tc.psum_pool(name="psum", bufs=8))
         ctx.enter_context(tc.manual_schedule())
 
         warm_in = const.tile([P, 8], F32, name="warm_in")
@@ -146,8 +144,10 @@ def tile_selfattention_pa_kernel(tc, x_words, x_scales, Wqk_words, Wqk_scales, b
         spread_bias(1)
 
         pending = []
-        warm_ps = psum_warm.tile([P, BANK], F32, name="warm_ps")
-        n_mx = 0
+        o_all = []
+        for i in range(2):
+            o_half = outp.tile([P, NCOLS // 2], F32, name="o_half%d" % i)
+            o_all.append(o_half)
 
         def rotate_and_store(c0, accs):
             nb = len(accs)
@@ -173,17 +173,17 @@ def tile_selfattention_pa_kernel(tc, x_words, x_scales, Wqk_words, Wqk_scales, b
                 nc.vector.tensor_tensor(out=w[:, 0:n], in0=u[:, 0:n], in1=sin_t[:, 0:n], op=MULT)
                 prods.append((col, v, w))
             for col, v, w in prods:
-                o = outp.tile([P, n], F32, name="o%d" % col)
+                which = col // (NCOLS // 2)
+                off = col % (NCOLS // 2)
+                o = o_all[which][:, off : off + n]
                 v4 = v[:, 0:n].rearrange("p (h s f) -> p h s f", s=2, f=HALF)
                 w4 = w[:, 0:n].rearrange("p (h s f) -> p h s f", s=2, f=HALF)
                 o4 = o[:, 0:n].rearrange("p (h s f) -> p h s f", s=2, f=HALF)
                 nc.vector.tensor_tensor(out=o4[:, :, 0, :], in0=v4[:, :, 0, :], in1=w4[:, :, 1, :], op=ADD)
                 nc.vector.tensor_tensor(out=o4[:, :, 1, :], in0=v4[:, :, 1, :], in1=w4[:, :, 0, :], op=ADD)
-                dst = outs[col // (NCOLS // 2)]
-                h0 = (col % (NCOLS // 2)) // HEAD
-                n_h = n // HEAD
-                for h in range(n_h):
-                    pending.append((dst[:, h0 + h, :, :].rearrange("b t f -> t b f"), o[:, HEAD * h : HEAD * (h + 1)]))
+                if which == 1:
+                    for h in range(n // HEAD):
+                        pending.append((out_1[:, off // HEAD + h, :, :].rearrange("b t f -> t b f"), o[:, HEAD * h : HEAD * (h + 1)]))
 
         for s in range(N_SUPER):
             if s + 2 < N_SUPER:
@@ -211,17 +211,9 @@ def tile_selfattention_pa_kernel(tc, x_words, x_scales, Wqk_words, Wqk_scales, b
                                 start=(g == 0),
                                 stop=(g == PASSES - 1),
                             )
-                            n_mx += 1
-                            if n_mx % 4 == 0:
-                                nc.tensor.matmul(
-                                    out=warm_ps[:, 0:HEAD],
-                                    lhsT=cos_t[:, 0:P],
-                                    rhs=cos_t[:, 0:HEAD],
-                                    start=True,
-                                    stop=True,
-                                )
                         g += 1
                 rotate_and_store(SUPER * s + BANK * b0, accs)
 
+        nc.sync.dma_start(out=out_0.rearrange("b h t f -> t (b h) f"), in_=o_all[0][:])
         for dst_ap, src_ap in pending:
             nc.sync.dma_start(out=dst_ap, in_=src_ap)

from contextlib import ExitStack

import concourse.mybir as mybir
from concourse.masks import make_identity

FLOPS = 2 * 128 * 4096 * 8192

F32 = mybir.dt.float32
BF16 = mybir.dt.bfloat16
I32 = mybir.dt.int32
U8 = mybir.dt.uint8
FP4X4 = mybir.dt.float4_e2m1fn_x4
ADD = mybir.AluOpType.add
MULT = mybir.AluOpType.mult

P = 128
PASSES = 8
BANK = 512
HALF = 128
HEAD = 256
NCOLS = 8192
SUPER = 2048
N_SUPER = NCOLS // SUPER
N_SLOTS = 3
UNIT = 1024
CHUNK_BYTES = 8192

SUBGROUPS = (
    ((0, 4, (2, 2, 2, 2)),),
    ((0, 4, (2, 2, 2, 2)),),
    ((0, 4, (2, 2, 2, 2)),),
    ((0, 1, (8,)), (1, 1, (8,)), (2, 1, (8,)), (3, 1, (4, 3, 1))),
)


def tile_selfattention_pa_kernel(tc, x_words, x_scales, Wqk_words, Wqk_scales, bqk, cos, sin, out_0, out_1):
    nc = tc.nc

    with ExitStack() as ctx:
        const = ctx.enter_context(tc.tile_pool(name="const", bufs=1))
        codes_pool = ctx.enter_context(tc.tile_pool(name="codes", bufs=8))
        work = ctx.enter_context(tc.tile_pool(name="work", bufs=2))
        outp = ctx.enter_context(tc.tile_pool(name="outp", bufs=1))
        psum = ctx.enter_context(tc.psum_pool(name="psum", bufs=8))
        ctx.enter_context(tc.manual_schedule())

        warm_in = const.tile([P, 8], F32, name="warm_in")
        warm_out = const.tile([P, 8], F32, name="warm_out")
        x_codes_in = const.tile([P, PASSES, 2 * P], U8, name="x_codes_in", align_bytes=64)
        x_plane_in = const.tile([P, PASSES, P], U8, name="x_plane_in", align_bytes=64)
        x_codes = const.tile([P, PASSES, 2 * P], U8, name="x_codes", align_bytes=64)
        x_plane = const.tile([P, PASSES, P], U8, name="x_plane", align_bytes=64)
        slots = []
        for i in range(N_SLOTS):
            slot = const.tile([P, PASSES, SUPER], U8, name="slot%d" % i, align_bytes=64)
            slots.append(slot)
        bias_rows = const.tile([P, BANK], BF16, name="bias_rows")
        ident = const.tile([P, P], BF16, name="ident")
        cs = const.tile([P, 2, HALF], BF16, name="cs")
        cos_t = const.tile([P, UNIT], F32, name="cos_t")
        sin_t = const.tile([P, UNIT], F32, name="sin_t")
        bias_sb = const.tile([P, NCOLS], BF16, name="bias_sb")

        def load_scales(plane, src, c0, width):
            for r in range(4):
                nc.sync.dma_start(
                    out=plane[r:P:32, :, 0:width].bitcast(I32),
                    in_=src[:, r:16:4, c0 : c0 + width].rearrange("g q n -> q g n").bitcast(I32),
                )

        def load_codes(c0, width, g0, n_g):
            ct = codes_pool.tile([P, CHUNK_BYTES], U8, name="ct", tag="ct", align_bytes=64)
            view = ct[:, 0 : n_g * 2 * width].rearrange("p (g c) -> p g c", g=n_g)
            nc.sync.dma_start(
                out=view.bitcast(I32),
                in_=Wqk_words[g0 : g0 + n_g, :, 2 * c0 : 2 * (c0 + width)].rearrange("g p c -> p g c").bitcast(I32),
            )
            return view

        loaded = {}

        def load_super(s, first_chunk_done):
            load_scales(slots[s % N_SLOTS], Wqk_scales, SUPER * s, SUPER)
            for q, (b0, nb, chunks) in enumerate(SUBGROUPS[s]):
                g0 = 0
                for ci, n_g in enumerate(chunks):
                    if not (first_chunk_done and q == 0 and ci == 0):
                        loaded[(s, q, ci)] = load_codes(SUPER * s + BANK * b0, BANK * nb, g0, n_g)
                    g0 += n_g

        nc.vector.memset(warm_in[:], 0.0)
        nc.scalar.copy(out=warm_out[:], in_=warm_in[:])
        nc.vector.memset(x_plane_in[:].bitcast(I32), 0)
        nc.vector.memset(slots[0][:].bitcast(I32), 0)
        nc.gpsimd.memset(bias_rows[:], 0.0)
        make_identity(nc, ident[:])
        nc.gpsimd.memset(slots[1][:].bitcast(F32), 0.0)
        nc.gpsimd.memset(slots[2][:].bitcast(F32), 0.0)

        nc.scalar.dma_start(out=bias_rows[0:16, :], in_=bqk.rearrange("(j n) -> j n", n=BANK))
        for b in range(2):
            nc.scalar.dma_start(out=cs[b:P:2, 0, :], in_=cos)
            nc.scalar.dma_start(out=cs[b:P:2, 1, :], in_=sin)

        nc.sync.dma_start(out=x_codes_in[:].bitcast(I32), in_=x_words.rearrange("g p c -> p g c").bitcast(I32))
        b0, nb, chunks = SUBGROUPS[0][0]
        loaded[(0, 0, 0)] = load_codes(BANK * b0, BANK * nb, 0, chunks[0])
        load_scales(x_plane_in, x_scales, 0, P)
        load_super(0, True)
        load_super(1, False)

        for b in range(2):
            nc.vector.tensor_copy(
                out=x_codes[:].rearrange("p g (t b e) -> p g t b e", b=2, e=2)[:, :, :, b, :],
                in_=x_codes_in[:].rearrange("p g (b t e) -> p g b t e", b=2, e=2)[:, :, b, :, :],
            )
            nc.vector.tensor_copy(
                out=x_plane[:].rearrange("p g (t b) -> p g t b", b=2)[:, :, :, b],
                in_=x_plane_in[:].rearrange("p g (b t) -> p g b t", b=2)[:, :, b, :],
            )

        nc.vector.tensor_copy(out=cos_t[:, 0:HALF], in_=cs[:, 0, :])
        nc.vector.tensor_copy(out=sin_t[:, 0:HALF], in_=cs[:, 1, :])
        nc.vector.tensor_copy(out=cos_t[:, HALF:HEAD], in_=cs[:, 0, :])
        nc.vector.tensor_scalar_mul(out=sin_t[:, HALF:HEAD], in0=cs[:, 1, :], scalar1=-1.0)
        for n in (HEAD, 2 * HEAD):
            nc.vector.tensor_copy(out=cos_t[:, n : 2 * n], in_=cos_t[:, 0:n])
            nc.vector.tensor_copy(out=sin_t[:, n : 2 * n], in_=sin_t[:, 0:n])

        def spread_bias(m):
            bp = psum.tile([P, 2 * BANK], BF16, name="bp", tag="bank")
            for e in range(2):
                j = 2 * m + e
                nc.tensor.matmul(
                    out=bp[:, BANK * e : BANK * (e + 1)],
                    lhsT=ident[:, j : j + 1].to_broadcast([P, P]),
                    rhs=bias_rows[:],
                    start=True,
                    stop=True,
                )
            nc.scalar.copy(out=bias_sb[:, 2 * BANK * m : 2 * BANK * (m + 1)], in_=bp[:])

        spread_bias(0)
        spread_bias(1)

        pending = []
        o_all = []
        for i in range(2):
            o_half = outp.tile([P, NCOLS // 2], F32, name="o_half%d" % i)
            o_all.append(o_half)

        def rotate_and_store(c0, accs):
            nb = len(accs)
            per_unit = 2 if nb == 4 else 1
            units = []
            for k0 in range(0, nb, per_unit):
                u = work.tile([P, UNIT], F32, name="u", tag="u")
                for k in range(per_unit):
                    col = c0 + BANK * (k0 + k)
                    nc.vector.tensor_tensor(
                        out=u[:, BANK * k : BANK * (k + 1)],
                        in0=accs[k0 + k][:],
                        in1=bias_sb[:, col : col + BANK],
                        op=ADD,
                    )
                units.append((c0 + BANK * k0, u))
            n = BANK * per_unit
            prods = []
            for col, u in units:
                v = work.tile([P, UNIT], F32, name="v", tag="v")
                w = work.tile([P, UNIT], F32, name="w", tag="w")
                nc.vector.tensor_tensor(out=v[:, 0:n], in0=u[:, 0:n], in1=cos_t[:, 0:n], op=MULT)
                nc.vector.tensor_tensor(out=w[:, 0:n], in0=u[:, 0:n], in1=sin_t[:, 0:n], op=MULT)
                prods.append((col, v, w))
            for col, v, w in prods:
                which = col // (NCOLS // 2)
                off = col % (NCOLS // 2)
                o = o_all[which][:, off : off + n]
                v4 = v[:, 0:n].rearrange("p (h s f) -> p h s f", s=2, f=HALF)
                w4 = w[:, 0:n].rearrange("p (h s f) -> p h s f", s=2, f=HALF)
                o4 = o[:, 0:n].rearrange("p (h s f) -> p h s f", s=2, f=HALF)
                nc.vector.tensor_tensor(out=o4[:, :, 0, :], in0=v4[:, :, 0, :], in1=w4[:, :, 1, :], op=ADD)
                nc.vector.tensor_tensor(out=o4[:, :, 1, :], in0=v4[:, :, 1, :], in1=w4[:, :, 0, :], op=ADD)
                if which == 1:
                    for h in range(n // HEAD):
                        pending.append((out_1[:, off // HEAD + h, :, :].rearrange("b t f -> t b f"), o[:, HEAD * h : HEAD * (h + 1)]))

        for s in range(N_SUPER):
            if s + 2 < N_SUPER:
                load_super(s + 2, False)
            plane = slots[s % N_SLOTS]
            for q, (b0, nb, chunks) in enumerate(SUBGROUPS[s]):
                if q == 0 and s + 1 < N_SUPER:
                    spread_bias(2 * s + 2)
                    spread_bias(2 * s + 3)
                accs = []
                for k in range(nb):
                    acc = psum.tile([P, BANK], F32, name="acc", tag="bank")
                    accs.append(acc)
                g = 0
                for ci, n_g in enumerate(chunks):
                    view = loaded[(s, q, ci)]
                    for gi in range(n_g):
                        for k in range(nb):
                            nc.tensor.matmul_mx(
                                out=accs[k][:],
                                lhsT=x_codes[:, g, :].bitcast(FP4X4),
                                lhsT_scale=x_plane[:, g, :],
                                rhs=view[:, gi, 2 * BANK * k : 2 * BANK * (k + 1)].bitcast(FP4X4),
                                rhs_scale=plane[:, g, BANK * (b0 + k) : BANK * (b0 + k + 1)],
                                start=(g == 0),
                                stop=(g == PASSES - 1),
                            )
                        g += 1
                rotate_and_store(SUPER * s + BANK * b0, accs)

        nc.sync.dma_start(out=out_0.rearrange("b h t f -> t (b h) f"), in_=o_all[0][:])
        for dst_ap, src_ap in pending:
            nc.sync.dma_start(out=dst_ap, in_=src_ap)
